import numpy as np
import ml_dtypes


def mxq(x, axis, fmt="e4m3"):
    dtype, down = {"e4m3": (ml_dtypes.float8_e4m3fn, 7), "e5m2": (ml_dtypes.float8_e5m2, 14)}[fmt]
    v = np.moveaxis(np.asarray(x, np.float32).astype(ml_dtypes.bfloat16).astype(np.float64), axis, -1)
    blocks = v.reshape(v.shape[:-1] + (-1, 32))
    amax = np.abs(blocks).max(-1, keepdims=True)
    byte = np.maximum(np.where(amax > 0, np.frexp(amax)[1] - 1 + 127, 0) - down, 1)
    scale = np.exp2(byte - 127.0)
    codes = (blocks / scale).astype(np.float32).astype(dtype).astype(np.float64)
    return np.moveaxis((codes * scale).reshape(v.shape), -1, axis)


WIDE = False


def mx_kscale(k):
    if not WIDE:
        return np.ones(k)
    levels = np.array([10, -10, 5, -5, 0])
    a = np.random.permutation(np.resize(levels, k // 512 * 4)).reshape(k // 512, 4)
    idx = np.arange(k)
    return np.exp2(a[idx // 512, idx % 128 // 32])


BF16 = ml_dtypes.bfloat16


def bf(x):
    return np.asarray(x, np.float32).astype(BF16)


def f64(x):
    return np.asarray(x).astype(np.float64)


E2M1 = np.array([0.0, 0.5, 1.0, 1.5, 2.0, 3.0, 4.0, 6.0, -0.0, -0.5, -1.0, -1.5, -2.0, -3.0, -4.0, -6.0])


def pack_weight(w, fmt):
    k, n = w.shape
    w = f64(bf(w)).reshape(k // 32, 32, n)
    amax = np.abs(w).max(1)
    if fmt == "e4m3":
        byte = np.frexp(amax)[1] - 1 + 127 - 7
    else:
        mant, ex = np.frexp(amax / 6.0)
        byte = np.where(mant > 0.5, ex, ex - 1) + 127
    byte = np.clip(np.where(amax > 0, byte, 1), 1, 254)
    scaled = (w * np.exp2(127.0 - byte)[:, None, :]).reshape(k, n).astype(np.float32)
    by_word = np.ascontiguousarray(scaled.reshape(k // 512, 128, 4, n).transpose(0, 1, 3, 2))
    if fmt == "e4m3":
        words = by_word.astype(ml_dtypes.float8_e4m3fn).view(np.uint8)
    else:
        c = by_word.astype(ml_dtypes.float4_e2m1fn).view(np.uint8) & 0xF
        words = c[..., 0::2] | (c[..., 1::2] << 4)
    return np.ascontiguousarray(words), np.ascontiguousarray(byte.astype(np.uint8).reshape(k // 512, 16, n))


def unpack_weight(words, scales, fmt):
    g, p, n, _ = words.shape
    if fmt == "e4m3":
        vals = np.ascontiguousarray(words).view(ml_dtypes.float8_e4m3fn).astype(np.float64)
    else:
        nib = np.empty((g, p, n, 4), np.uint8)
        nib[..., 0::2] = words & 0xF
        nib[..., 1::2] = words >> 4
        vals = E2M1[nib]
    vals = vals * np.repeat(np.exp2(scales.astype(np.float64) - 127.0), 8, axis=1)[..., None]
    return vals.transpose(0, 1, 3, 2).reshape(g * 512, n)


B, D, U = 2048, 512, 128
FMT = "e4m3"


def sigmoid(v):
    return 1.0 / (1.0 + np.exp(-v))


def setup_inputs():
    s = mx_kscale(D)
    inp = {"pre_layer": bf(np.random.standard_normal((2, B, U))), "x": bf(np.random.standard_normal((B, D)) * s)}
    for n in ("W_i", "W_f", "W_o", "W_c"):
        words, scales = pack_weight(np.random.standard_normal((D, U)) / np.sqrt(D) / s[:, None], FMT)
        inp[n + "_words"] = words
        inp[n + "_scales"] = scales
    for n in ("U_i", "U_f", "U_o", "U_c"):
        inp[n] = bf(np.random.standard_normal((U, U)) / np.sqrt(U))
    return inp


def reference(pre_layer, x, W_i_words, W_i_scales, W_f_words, W_f_scales, W_o_words, W_o_scales, W_c_words, W_c_scales, U_i, U_f, U_o, U_c):
    pre = f64(pre_layer)
    pre_h, pre_c = pre[0], pre[1]
    W = np.concatenate([unpack_weight(W_i_words, W_i_scales, FMT), unpack_weight(W_f_words, W_f_scales, FMT),
                        unpack_weight(W_o_words, W_o_scales, FMT), unpack_weight(W_c_words, W_c_scales, FMT)], axis=1)
    Uw = np.concatenate([f64(U_i), f64(U_f), f64(U_o), f64(U_c)], axis=1)
    gates = (mxq(f64(x), 1, "e4m3") @ W) + pre_h @ Uw
    zi, zf, zo, zc = np.split(gates, 4, axis=1)
    i_t = sigmoid(zi)
    f_t = sigmoid(zf)
    o_t = sigmoid(zo)
    n_c_t = np.tanh(zc)
    c = f_t * pre_c + i_t * n_c_t
    h = o_t * np.tanh(c)
    return np.stack([h, c])

@@ -1,0 +1,209 @@
+from contextlib import ExitStack
+
+import concourse.mybir as mybir
+from concourse.masks import make_identity
+
+F32 = mybir.dt.float32
+BF16 = mybir.dt.bfloat16
+I32 = mybir.dt.int32
+U32 = mybir.dt.uint32
+U8 = mybir.dt.uint8
+FP8X4 = mybir.dt.float8_e4m3fn_x4
+ACT = mybir.ActivationFunctionType
+ALU = mybir.AluOpType
+
+P = 128
+B, D, U = 2048, 512, 128
+GATES = 4
+Z = GATES * U
+TILES = B // P
+UNIT = 2
+UNITS = TILES // UNIT
+CHUNK = 4
+AHEAD = 4
+
+FLOPS = 2 * B * D * Z + 2 * B * U * Z
+
+
+def tile_lstm_kernel(
+    tc,
+    pre_layer,
+    x,
+    W_i_words,
+    W_i_scales,
+    W_f_words,
+    W_f_scales,
+    W_o_words,
+    W_o_scales,
+    W_c_words,
+    W_c_scales,
+    U_i,
+    U_f,
+    U_o,
+    U_c,
+    out,
+):
+    nc = tc.nc
+    w_words_in = [W_i_words, W_f_words, W_o_words, W_c_words]
+    w_scales_in = [W_i_scales, W_f_scales, W_o_scales, W_c_scales]
+    u_in = [U_i, U_f, U_o, U_c]
+
+    x_view = x.rearrange("(p t) k -> p t k", t=TILES)
+    pre_h_view = pre_layer[0].rearrange("(p t) u -> p t u", t=TILES)
+    pre_c_view = pre_layer[1].rearrange("(p t) u -> p t u", t=TILES)
+    h_view = out[0].rearrange("(p t) u -> p t u", t=TILES)
+    c_view = out[1].rearrange("(p t) u -> p t u", t=TILES)
+
+    with ExitStack() as ctx:
+        ctx.enter_context(tc.manual_schedule())
+        keep = ctx.enter_context(tc.tile_pool(name="keep", bufs=1))
+        psum = ctx.enter_context(tc.psum_pool(name="psum", bufs=1))
+
+        def per_unit(shape, dtype, name):
+            return [keep.tile(shape, dtype, name="%s%d" % (name, n), align_bytes=64) for n in range(UNITS)]
+
+        x_sb = [keep.tile([P, CHUNK, D], BF16, name="x_sb%d" % n) for n in range(TILES // CHUNK)]
+        grouped = per_unit([P, UNIT, P, 4], BF16, "grouped")
+        x_codes = per_unit([P, UNIT * P], U32, "x_codes")
+        x_plane = per_unit([P, UNIT * P], U8, "x_plane")
+        pre_h_t = per_unit([P, UNIT, P], BF16, "pre_h_t")
+        z_sb = per_unit([P, UNIT, Z], F32, "z_sb")
+        kept = per_unit([P, UNIT, U], F32, "kept")
+        fresh = per_unit([P, UNIT, U], F32, "fresh")
+        c_sb = per_unit([P, UNIT, U], F32, "c_sb")
+        tanh_c = per_unit([P, UNIT, U], F32, "tanh_c")
+        h_sb = per_unit([P, UNIT, U], F32, "h_sb")
+        xt_ps = {}
+        ht_ps = {}
+        zp_ps = {}
+        zm_ps = {}
+
+        pre_h_sb = keep.tile([P, TILES, U], BF16)
+        pre_c_sb = keep.tile([P, TILES, U], BF16)
+        u_sb = keep.tile([P, Z], BF16)
+        w_words = keep.tile([P, Z], U32, align_bytes=64)
+        w_plane = keep.tile([P, Z], U8, align_bytes=64)
+        ident_f32 = keep.tile([P, P], F32)
+        ident_bf16 = keep.tile([P, P], BF16)
+        warm = keep.tile([P, 2], F32)
+
+        def tiles_of(n):
+            return slice(n * UNIT, (n + 1) * UNIT)
+
+        def load_x(queue, n):
+            queue.dma_start(out=x_sb[n][:], in_=x_view[:, n * CHUNK : (n + 1) * CHUNK, :])
+
+        nc.vector.memset(w_plane[:].bitcast(I32), 0)
+        nc.vector.memset(warm[:, 0:1], 0.0)
+        load_x(nc.scalar, 0)
+        for gate in range(GATES):
+            nc.scalar.dma_start(out=u_sb[:, gate * U : (gate + 1) * U], in_=u_in[gate])
+        nc.scalar.activation(out=warm[:, 1:2], in_=warm[:, 0:1], func=ACT.Sigmoid)
+        make_identity(nc, ident_f32[:])
+        nc.gpsimd.dma_start(out=pre_h_sb[:], in_=pre_h_view)
+        make_identity(nc, ident_bf16[:])
+        for n in range(1, TILES // CHUNK):
+            load_x(nc.gpsimd, n)
+        nc.gpsimd.dma_start(out=pre_c_sb[:], in_=pre_c_view)
+        for gate in range(GATES):
+            cols = slice(gate * U, (gate + 1) * U)
+            rows = w_scales_in[gate].rearrange("o (q r) n -> r (o q) n", r=4).bitcast(I32)
+            for r in range(4):
+                nc.sync.dma_start(out=w_plane[r:P:32, cols].bitcast(I32), in_=rows[r])
+        for gate in range(GATES):
+            cols = slice(gate * U, (gate + 1) * U)
+            nc.sync.dma_start(
+                out=w_words[:, cols].bitcast(I32),
+                in_=w_words_in[gate].rearrange("o p n t -> (o p) (n t)").bitcast(I32),
+            )
+
+        def transposes(n):
+            xt_ps[n] = psum.tile([P, UNIT, 2, P], F32, name="xt%d" % n, tag="xt", bufs=2)
+            for j in range(UNIT):
+                t = n * UNIT + j
+                words = x_sb[t // CHUNK][:, t % CHUNK, :].bitcast(F32)
+                for u in range(2):
+                    nc.tensor.transpose(xt_ps[n][:, j, u, :], words[:, u : D // 2 : 2], ident_f32[:])
+            ht_ps[n] = psum.tile([P, UNIT, P], BF16, name="ht%d" % n, tag="ht", bufs=1)
+            for j in range(UNIT):
+                nc.tensor.transpose(ht_ps[n][:, j, :], pre_h_sb[:, n * UNIT + j, :], ident_bf16[:])
+
+        def copy_x_t(n):
+            nc.vector.tensor_copy(out=grouped[n][:].bitcast(F32), in_=xt_ps[n][:].rearrange("p j u b -> p j b u"))
+
+        def copy_h_t(n):
+            nc.scalar.copy(out=pre_h_t[n][:], in_=ht_ps[n][:])
+
+        def quantise(n):
+            nc.vector.quantize_mx(
+                out=x_codes[n][:].bitcast(FP8X4),
+                scales=x_plane[n][:],
+                in_=grouped[n][:].rearrange("p j b t -> p (j b t)"),
+            )
+
+        def plain_products(n):
+            for j in range(UNIT):
+                zp_ps[n, j] = psum.tile([P, Z], F32, name="zp%d_%d" % (n, j), tag="zp", bufs=2)
+                nc.tensor.matmul(out=zp_ps[n, j][:], lhsT=pre_h_t[n][:, j, :], rhs=u_sb[:], start=True, stop=True)
+
+        def copy_plain(n):
+            for j in range(UNIT):
+                nc.scalar.copy(out=z_sb[n][:, j, :], in_=zp_ps[n, j][:])
+
+        def mx_products(n):
+            for j in range(UNIT):
+                cols = slice(j * P, (j + 1) * P)
+                zm_ps[n, j] = psum.tile([P, Z], F32, name="zm%d_%d" % (n, j), tag="zm", bufs=3)
+                nc.tensor.matmul_mx(
+                    out=zm_ps[n, j][:],
+                    lhsT=x_codes[n][:, cols].bitcast(FP8X4),
+                    lhsT_scale=x_plane[n][:, cols],
+                    rhs=w_words[:].bitcast(FP8X4),
+                    rhs_scale=w_plane[:],
+                    start=True,
+                    stop=True,
+                )
+
+        def add_products(n):
+            for j in range(UNIT):
+                nc.vector.tensor_tensor(out=z_sb[n][:, j, :], in0=zm_ps[n, j][:], in1=z_sb[n][:, j, :], op=ALU.add)
+
+        def gate_functions(n):
+            z = z_sb[n]
+            nc.scalar.activation(out=z[:, :, 0 : 3 * U], in_=z[:, :, 0 : 3 * U], func=ACT.Sigmoid)
+            nc.scalar.activation(out=z[:, :, 3 * U : Z], in_=z[:, :, 3 * U : Z], func=ACT.Tanh)
+
+        def two_products(n):
+            z = z_sb[n]
+            nc.gpsimd.tensor_tensor(out=kept[n][:], in0=z[:, :, U : 2 * U], in1=pre_c_sb[:, tiles_of(n), :], op=ALU.mult)
+            nc.gpsimd.tensor_tensor(out=fresh[n][:], in0=z[:, :, 0:U], in1=z[:, :, 3 * U : Z], op=ALU.mult)
+
+        def new_c(n):
+            nc.vector.tensor_tensor(out=c_sb[n][:], in0=kept[n][:], in1=fresh[n][:], op=ALU.add)
+            nc.sync.dma_start(out=c_view[:, tiles_of(n), :], in_=c_sb[n][:])
+
+        def tanh_of_c(n):
+            nc.scalar.activation(out=tanh_c[n][:], in_=c_sb[n][:], func=ACT.Tanh)
+
+        def new_h(n):
+            nc.vector.tensor_tensor(out=h_sb[n][:], in0=z_sb[n][:, :, 2 * U : 3 * U], in1=tanh_c[n][:], op=ALU.mult)
+            nc.sync.dma_start(out=h_view[:, tiles_of(n), :], in_=h_sb[n][:])
+
+        def stage(work, n):
+            if 0 <= n < UNITS:
+                work(n)
+
+        for i in range(UNITS + AHEAD + 4):
+            stage(transposes, i)
+            stage(plain_products, i - 1)
+            stage(mx_products, i - AHEAD)
+            stage(gate_functions, i - AHEAD - 1)
+            stage(two_products, i - AHEAD - 1)
+            stage(copy_x_t, i)
+            stage(copy_h_t, i)
+            stage(quantise, i - 1)
+            stage(copy_plain, i - 1)
+            stage(add_products, i - AHEAD)
+            stage(new_c, i - AHEAD - 2)
+            stage(tanh_of_c, i - AHEAD - 2)
+            stage(new_h, i - AHEAD - 3)

@@ -90,32 +90,43 @@ def tile_lstm_kernel(
         def tiles_of(n):
             return slice(n * UNIT, (n + 1) * UNIT)
 
-        def load_x(queue, n):
-            queue.dma_start(out=x_sb[n][:], in_=x_view[:, n * CHUNK : (n + 1) * CHUNK, :])
+        def load_x(n):
+            nc.gpsimd.dma_start(out=x_sb[n][:], in_=x_view[:, n * CHUNK : (n + 1) * CHUNK, :])
+
+        def load_scale_rows(queue, view, gate):
+            cols = slice(gate * U, (gate + 1) * U)
+            rows = w_scales_in[gate].rearrange("o (q r) n -> r (o q) n", r=4).bitcast(view)
+            for r in range(4):
+                queue.dma_start(out=w_plane[r:P:32, cols].bitcast(view), in_=rows[r])
+
+        def load_words(queue, view, gate):
+            cols = slice(gate * U, (gate + 1) * U)
+            queue.dma_start(
+                out=w_words[:, cols].bitcast(view),
+                in_=w_words_in[gate].rearrange("o p n t -> (o p) (n t)").bitcast(view),
+            )
 
         nc.vector.memset(w_plane[:].bitcast(I32), 0)
         nc.vector.memset(warm[:, 0:1], 0.0)
-        load_x(nc.scalar, 0)
-        for gate in range(GATES):
-            nc.scalar.dma_start(out=u_sb[:, gate * U : (gate + 1) * U], in_=u_in[gate])
-        nc.scalar.activation(out=warm[:, 1:2], in_=warm[:, 0:1], func=ACT.Sigmoid)
-        make_identity(nc, ident_f32[:])
+        load_x(0)
         nc.gpsimd.dma_start(out=pre_h_sb[:], in_=pre_h_view)
+        make_identity(nc, ident_f32[:])
         make_identity(nc, ident_bf16[:])
         for n in range(1, TILES // CHUNK):
-            load_x(nc.gpsimd, n)
+            load_x(n)
         nc.gpsimd.dma_start(out=pre_c_sb[:], in_=pre_c_view)
+
         for gate in range(GATES):
-            cols = slice(gate * U, (gate + 1) * U)
-            rows = w_scales_in[gate].rearrange("o (q r) n -> r (o q) n", r=4).bitcast(I32)
-            for r in range(4):
-                nc.sync.dma_start(out=w_plane[r:P:32, cols].bitcast(I32), in_=rows[r])
-        for gate in range(GATES):
-            cols = slice(gate * U, (gate + 1) * U)
-            nc.sync.dma_start(
-                out=w_words[:, cols].bitcast(I32),
-                in_=w_words_in[gate].rearrange("o p n t -> (o p) (n t)").bitcast(I32),
-            )
+            nc.scalar.dma_start(out=u_sb[:, gate * U : (gate + 1) * U], in_=u_in[gate])
+        load_scale_rows(nc.sync, I32, 0)
+        load_scale_rows(nc.scalar, F32, 2)
+        load_scale_rows(nc.sync, I32, 1)
+        load_scale_rows(nc.scalar, F32, 3)
+        load_words(nc.sync, I32, 0)
+        load_words(nc.sync, I32, 1)
+        load_words(nc.scalar, F32, 2)
+        load_words(nc.scalar, F32, 3)
+        nc.scalar.activation(out=warm[:, 1:2], in_=warm[:, 0:1], func=ACT.Sigmoid)
 
         def transposes(n):
             xt_ps[n] = psum.tile([P, UNIT, 2, P], F32, name="xt%d" % n, tag="xt", bufs=2)

@@ -20,7 +20,11 @@ TILES = B // P
 UNIT = 2
 UNITS = TILES // UNIT
 CHUNK = 4
-AHEAD = 4
+H_TILES = 8
+AHEAD = 5
+LAG_GATES = 1
+LAG_C = 4
+LAG_H = 5
 
 FLOPS = 2 * B * D * Z + 2 * B * U * Z
 
@@ -66,7 +70,7 @@ def tile_lstm_kernel(
         grouped = per_unit([P, UNIT, P, 4], BF16, "grouped")
         x_codes = per_unit([P, UNIT * P], U32, "x_codes")
         x_plane = per_unit([P, UNIT * P], U8, "x_plane")
-        pre_h_t = per_unit([P, UNIT, P], BF16, "pre_h_t")
+        pre_h_t = [keep.tile([P, H_TILES, P], BF16, name="pre_h_t%d" % n) for n in range(TILES // H_TILES)]
         z_sb = per_unit([P, UNIT, Z], F32, "z_sb")
         kept = per_unit([P, UNIT, U], F32, "kept")
         fresh = per_unit([P, UNIT, U], F32, "fresh")
@@ -90,43 +94,34 @@ def tile_lstm_kernel(
         def tiles_of(n):
             return slice(n * UNIT, (n + 1) * UNIT)
 
-        def load_x(n):
-            nc.gpsimd.dma_start(out=x_sb[n][:], in_=x_view[:, n * CHUNK : (n + 1) * CHUNK, :])
-
-        def load_scale_rows(queue, view, gate):
-            cols = slice(gate * U, (gate + 1) * U)
-            rows = w_scales_in[gate].rearrange("o (q r) n -> r (o q) n", r=4).bitcast(view)
-            for r in range(4):
-                queue.dma_start(out=w_plane[r:P:32, cols].bitcast(view), in_=rows[r])
-
-        def load_words(queue, view, gate):
-            cols = slice(gate * U, (gate + 1) * U)
-            queue.dma_start(
-                out=w_words[:, cols].bitcast(view),
-                in_=w_words_in[gate].rearrange("o p n t -> (o p) (n t)").bitcast(view),
-            )
+        def load_x(queue, n):
+            queue.dma_start(out=x_sb[n][:], in_=x_view[:, n * CHUNK : (n + 1) * CHUNK, :])
 
         nc.vector.memset(w_plane[:].bitcast(I32), 0)
         nc.vector.memset(warm[:, 0:1], 0.0)
-        load_x(0)
-        nc.gpsimd.dma_start(out=pre_h_sb[:], in_=pre_h_view)
-        make_identity(nc, ident_f32[:])
-        make_identity(nc, ident_bf16[:])
-        for n in range(1, TILES // CHUNK):
-            load_x(n)
-        nc.gpsimd.dma_start(out=pre_c_sb[:], in_=pre_c_view)
-
+        nc.vector.memset(ident_f32[:], 0.0)
+        load_x(nc.sync, 0)
         for gate in range(GATES):
             nc.scalar.dma_start(out=u_sb[:, gate * U : (gate + 1) * U], in_=u_in[gate])
-        load_scale_rows(nc.sync, I32, 0)
-        load_scale_rows(nc.scalar, F32, 2)
-        load_scale_rows(nc.sync, I32, 1)
-        load_scale_rows(nc.scalar, F32, 3)
-        load_words(nc.sync, I32, 0)
-        load_words(nc.sync, I32, 1)
-        load_words(nc.scalar, F32, 2)
-        load_words(nc.scalar, F32, 3)
+        nc.scalar.dma_start(out=pre_h_sb[:], in_=pre_h_view)
+        load_x(nc.scalar, 1)
         nc.scalar.activation(out=warm[:, 1:2], in_=warm[:, 0:1], func=ACT.Sigmoid)
+        make_identity(nc, ident_f32[:], nomemset=True)
+        nc.vector.tensor_copy(out=ident_bf16[:], in_=ident_f32[:])
+        for n in range(2, TILES // CHUNK):
+            load_x(nc.gpsimd, n)
+        nc.gpsimd.dma_start(out=pre_c_sb[:], in_=pre_c_view)
+        for gate in range(GATES):
+            cols = slice(gate * U, (gate + 1) * U)
+            rows = w_scales_in[gate].rearrange("o (q r) n -> r (o q) n", r=4).bitcast(I32)
+            for r in range(4):
+                nc.sync.dma_start(out=w_plane[r:P:32, cols].bitcast(I32), in_=rows[r])
+        for gate in range(GATES):
+            cols = slice(gate * U, (gate + 1) * U)
+            nc.sync.dma_start(
+                out=w_words[:, cols].bitcast(I32),
+                in_=w_words_in[gate].rearrange("o p n t -> (o p) (n t)").bitcast(I32),
+            )
 
         def transposes(n):
             xt_ps[n] = psum.tile([P, UNIT, 2, P], F32, name="xt%d" % n, tag="xt", bufs=2)
@@ -135,15 +130,15 @@ def tile_lstm_kernel(
                 words = x_sb[t // CHUNK][:, t % CHUNK, :].bitcast(F32)
                 for u in range(2):
                     nc.tensor.transpose(xt_ps[n][:, j, u, :], words[:, u : D // 2 : 2], ident_f32[:])
-            ht_ps[n] = psum.tile([P, UNIT, P], BF16, name="ht%d" % n, tag="ht", bufs=1)
-            for j in range(UNIT):
-                nc.tensor.transpose(ht_ps[n][:, j, :], pre_h_sb[:, n * UNIT + j, :], ident_bf16[:])
+
+        def transposes_h(n):
+            ht_ps[n] = psum.tile([P, H_TILES, P], BF16, name="ht%d" % n, tag="ht", bufs=1)
+            for j in range(H_TILES):
+                nc.tensor.transpose(ht_ps[n][:, j, :], pre_h_sb[:, n * H_TILES + j, :], ident_bf16[:])
+            nc.scalar.copy(out=pre_h_t[n][:], in_=ht_ps[n][:])
 
         def copy_x_t(n):
             nc.vector.tensor_copy(out=grouped[n][:].bitcast(F32), in_=xt_ps[n][:].rearrange("p j u b -> p j b u"))
-
-        def copy_h_t(n):
-            nc.scalar.copy(out=pre_h_t[n][:], in_=ht_ps[n][:])
 
         def quantise(n):
             nc.vector.quantize_mx(
@@ -154,17 +149,23 @@ def tile_lstm_kernel(
 
         def plain_products(n):
             for j in range(UNIT):
-                zp_ps[n, j] = psum.tile([P, Z], F32, name="zp%d_%d" % (n, j), tag="zp", bufs=2)
-                nc.tensor.matmul(out=zp_ps[n, j][:], lhsT=pre_h_t[n][:, j, :], rhs=u_sb[:], start=True, stop=True)
+                t = n * UNIT + j
+                zp_ps[n, j] = psum.tile([P, Z], F32, name="zp%d_%d" % (n, j), tag="z", bufs=5)
+                nc.tensor.matmul(
+                    out=zp_ps[n, j][:], lhsT=pre_h_t[t // H_TILES][:, t % H_TILES, :], rhs=u_sb[:], start=True, stop=True
+                )
 
         def copy_plain(n):
             for j in range(UNIT):
-                nc.scalar.copy(out=z_sb[n][:, j, :], in_=zp_ps[n, j][:])
+                if (n * UNIT + j) % 4 == 3:
+                    nc.vector.tensor_copy(out=z_sb[n][:, j, :], in_=zp_ps[n, j][:])
+                else:
+                    nc.scalar.copy(out=z_sb[n][:, j, :], in_=zp_ps[n, j][:])
 
         def mx_products(n):
             for j in range(UNIT):
                 cols = slice(j * P, (j + 1) * P)
-                zm_ps[n, j] = psum.tile([P, Z], F32, name="zm%d_%d" % (n, j), tag="zm", bufs=3)
+                zm_ps[n, j] = psum.tile([P, Z], F32, name="zm%d_%d" % (n, j), tag="z", bufs=5)
                 nc.tensor.matmul_mx(
                     out=zm_ps[n, j][:],
                     lhsT=x_codes[n][:, cols].bitcast(FP8X4),
@@ -204,17 +205,19 @@ def tile_lstm_kernel(
             if 0 <= n < UNITS:
                 work(n)
 
-        for i in range(UNITS + AHEAD + 4):
+        for i in range(UNITS + AHEAD + LAG_H + 1):
+            n = i - AHEAD
             stage(transposes, i)
+            if i % (H_TILES // UNIT) == 0 and i < UNITS:
+                transposes_h(i * UNIT // H_TILES)
             stage(plain_products, i - 1)
-            stage(mx_products, i - AHEAD)
-            stage(gate_functions, i - AHEAD - 1)
-            stage(two_products, i - AHEAD - 1)
+            stage(mx_products, n)
+            stage(gate_functions, n - LAG_GATES)
+            stage(two_products, n - LAG_GATES)
             stage(copy_x_t, i)
-            stage(copy_h_t, i)
             stage(quantise, i - 1)
             stage(copy_plain, i - 1)
-            stage(add_products, i - AHEAD)
-            stage(new_c, i - AHEAD - 2)
-            stage(tanh_of_c, i - AHEAD - 2)
-            stage(new_h, i - AHEAD - 3)
+            stage(add_products, n)
+            stage(new_c, n - LAG_C)
+            stage(tanh_of_c, n - LAG_C)
+            stage(new_h, n - LAG_H)

@@ -21,10 +21,13 @@ UNIT = 2
 UNITS = TILES // UNIT
 CHUNK = 4
 H_TILES = 8
-AHEAD = 5
-LAG_GATES = 1
-LAG_C = 4
-LAG_H = 5
+AHEAD = 6
+H_STEPS = (1, 3)
+LAG_PLAIN = 2
+LAG_Z = 1
+LAG_GATES = 2
+LAG_C = 3
+LAG_H = 4
 
 FLOPS = 2 * B * D * Z + 2 * B * U * Z
 
@@ -71,6 +74,7 @@ def tile_lstm_kernel(
         x_codes = per_unit([P, UNIT * P], U32, "x_codes")
         x_plane = per_unit([P, UNIT * P], U8, "x_plane")
         pre_h_t = [keep.tile([P, H_TILES, P], BF16, name="pre_h_t%d" % n) for n in range(TILES // H_TILES)]
+        y_sb = per_unit([P, GATES, UNIT, P], F32, "y_sb")
         z_sb = per_unit([P, UNIT, Z], F32, "z_sb")
         kept = per_unit([P, UNIT, U], F32, "kept")
         fresh = per_unit([P, UNIT, U], F32, "fresh")
@@ -79,8 +83,9 @@ def tile_lstm_kernel(
         h_sb = per_unit([P, UNIT, U], F32, "h_sb")
         xt_ps = {}
         ht_ps = {}
+        y_ps = {}
+        z_ps = {}
         zp_ps = {}
-        zm_ps = {}
 
         pre_h_sb = keep.tile([P, TILES, U], BF16)
         pre_c_sb = keep.tile([P, TILES, U], BF16)
@@ -124,7 +129,7 @@ def tile_lstm_kernel(
             )
 
         def transposes(n):
-            xt_ps[n] = psum.tile([P, UNIT, 2, P], F32, name="xt%d" % n, tag="xt", bufs=2)
+            xt_ps[n] = psum.tile([P, UNIT, 2, P], F32, name="xt%d" % n, tag="a", bufs=4)
             for j in range(UNIT):
                 t = n * UNIT + j
                 words = x_sb[t // CHUNK][:, t % CHUNK, :].bitcast(F32)
@@ -132,7 +137,7 @@ def tile_lstm_kernel(
                     nc.tensor.transpose(xt_ps[n][:, j, u, :], words[:, u : D // 2 : 2], ident_f32[:])
 
         def transposes_h(n):
-            ht_ps[n] = psum.tile([P, H_TILES, P], BF16, name="ht%d" % n, tag="ht", bufs=1)
+            ht_ps[n] = psum.tile([P, H_TILES, P], BF16, name="ht%d" % n, tag="a", bufs=4)
             for j in range(H_TILES):
                 nc.tensor.transpose(ht_ps[n][:, j, :], pre_h_sb[:, n * H_TILES + j, :], ident_bf16[:])
             nc.scalar.copy(out=pre_h_t[n][:], in_=ht_ps[n][:])
@@ -147,27 +152,24 @@ def tile_lstm_kernel(
                 in_=grouped[n][:].rearrange("p j b t -> p (j b t)"),
             )
 
+        def by_copy(n):
+            return n % 3 == 1
+
         def plain_products(n):
             for j in range(UNIT):
                 t = n * UNIT + j
-                zp_ps[n, j] = psum.tile([P, Z], F32, name="zp%d_%d" % (n, j), tag="z", bufs=5)
+                zp_ps[n, j] = psum.tile([P, Z], F32, name="zp%d_%d" % (n, j), tag="z", bufs=4)
                 nc.tensor.matmul(
                     out=zp_ps[n, j][:], lhsT=pre_h_t[t // H_TILES][:, t % H_TILES, :], rhs=u_sb[:], start=True, stop=True
                 )
+                nc.scalar.copy(out=z_sb[n][:, j, :], in_=zp_ps[n, j][:])
 
-        def copy_plain(n):
-            for j in range(UNIT):
-                if (n * UNIT + j) % 4 == 3:
-                    nc.vector.tensor_copy(out=z_sb[n][:, j, :], in_=zp_ps[n, j][:])
-                else:
-                    nc.scalar.copy(out=z_sb[n][:, j, :], in_=zp_ps[n, j][:])
-
-        def mx_products(n):
+        def mx_products_rows(n):
             for j in range(UNIT):
                 cols = slice(j * P, (j + 1) * P)
-                zm_ps[n, j] = psum.tile([P, Z], F32, name="zm%d_%d" % (n, j), tag="z", bufs=5)
+                z_ps[n, j] = psum.tile([P, Z], F32, name="zm%d_%d" % (n, j), tag="z", bufs=4)
                 nc.tensor.matmul_mx(
-                    out=zm_ps[n, j][:],
+                    out=z_ps[n, j][:],
                     lhsT=x_codes[n][:, cols].bitcast(FP8X4),
                     lhsT_scale=x_plane[n][:, cols],
                     rhs=w_words[:].bitcast(FP8X4),
@@ -178,17 +180,68 @@ def tile_lstm_kernel(
 
         def add_products(n):
             for j in range(UNIT):
-                nc.vector.tensor_tensor(out=z_sb[n][:, j, :], in0=zm_ps[n, j][:], in1=z_sb[n][:, j, :], op=ALU.add)
+                nc.vector.tensor_tensor(out=z_sb[n][:, j, :], in0=z_ps[n, j][:], in1=z_sb[n][:, j, :], op=ALU.add)
+
+        def mx_products(n):
+            if by_copy(n):
+                mx_products_rows(n)
+                return
+            for half in range(GATES // 2):
+                y_ps[n, half] = psum.tile([P, 2, UNIT * P], F32, name="y%d_%d" % (n, half), tag="a", bufs=4)
+                for e in range(2):
+                    cols = slice((2 * half + e) * U, (2 * half + e + 1) * U)
+                    nc.tensor.matmul_mx(
+                        out=y_ps[n, half][:, e, :],
+                        lhsT=w_words[:, cols].bitcast(FP8X4),
+                        lhsT_scale=w_plane[:, cols],
+                        rhs=x_codes[n][:].bitcast(FP8X4),
+                        rhs_scale=x_plane[n][:],
+                        start=True,
+                        stop=True,
+                    )
+
+        def copy_mx(n):
+            if by_copy(n):
+                add_products(n)
+                return
+            for half in range(GATES // 2):
+                out = y_sb[n][:, 2 * half : 2 * half + 2, :, :].rearrange("p g j b -> p g (j b)")
+                nc.vector.tensor_copy(out=out, in_=y_ps[n, half][:])
+
+        def sums(n):
+            if by_copy(n):
+                return
+            for j in range(UNIT):
+                t = n * UNIT + j
+                z_ps[n, j] = psum.tile([P, Z], F32, name="z%d_%d" % (n, j), tag="z", bufs=4)
+                nc.tensor.matmul(
+                    out=z_ps[n, j][:], lhsT=pre_h_t[t // H_TILES][:, t % H_TILES, :], rhs=u_sb[:], start=True, stop=False
+                )
+                for gate in range(GATES):
+                    nc.tensor.matmul(
+                        out=z_ps[n, j][:, gate * U : (gate + 1) * U],
+                        lhsT=y_sb[n][:, gate, j, :],
+                        rhs=ident_f32[:],
+                        is_transpose=True,
+                        start=False,
+                        stop=(gate == GATES - 1),
+                    )
 
         def gate_functions(n):
-            z = z_sb[n]
-            nc.scalar.activation(out=z[:, :, 0 : 3 * U], in_=z[:, :, 0 : 3 * U], func=ACT.Sigmoid)
-            nc.scalar.activation(out=z[:, :, 3 * U : Z], in_=z[:, :, 3 * U : Z], func=ACT.Tanh)
+            if by_copy(n):
+                z = z_sb[n]
+                nc.scalar.activation(out=z[:, :, 0 : 3 * U], in_=z[:, :, 0 : 3 * U], func=ACT.Sigmoid)
+                nc.scalar.activation(out=z[:, :, 3 * U : Z], in_=z[:, :, 3 * U : Z], func=ACT.Tanh)
+                return
+            for j in range(UNIT):
+                nc.scalar.activation(out=z_sb[n][:, j, 0 : 3 * U], in_=z_ps[n, j][:, 0 : 3 * U], func=ACT.Sigmoid)
+                nc.scalar.activation(out=z_sb[n][:, j, 3 * U : Z], in_=z_ps[n, j][:, 3 * U : Z], func=ACT.Tanh)
 
         def two_products(n):
+            engine = nc.gpsimd if n < UNITS - 1 else nc.vector
             z = z_sb[n]
-            nc.gpsimd.tensor_tensor(out=kept[n][:], in0=z[:, :, U : 2 * U], in1=pre_c_sb[:, tiles_of(n), :], op=ALU.mult)
-            nc.gpsimd.tensor_tensor(out=fresh[n][:], in0=z[:, :, 0:U], in1=z[:, :, 3 * U : Z], op=ALU.mult)
+            engine.tensor_tensor(out=kept[n][:], in0=z[:, :, U : 2 * U], in1=pre_c_sb[:, tiles_of(n), :], op=ALU.mult)
+            engine.tensor_tensor(out=fresh[n][:], in0=z[:, :, 0:U], in1=z[:, :, 3 * U : Z], op=ALU.mult)
 
         def new_c(n):
             nc.vector.tensor_tensor(out=c_sb[n][:], in0=kept[n][:], in1=fresh[n][:], op=ALU.add)
@@ -208,16 +261,17 @@ def tile_lstm_kernel(
         for i in range(UNITS + AHEAD + LAG_H + 1):
             n = i - AHEAD
             stage(transposes, i)
-            if i % (H_TILES // UNIT) == 0 and i < UNITS:
-                transposes_h(i * UNIT // H_TILES)
-            stage(plain_products, i - 1)
+            if i in H_STEPS:
+                transposes_h(H_STEPS.index(i))
+            if by_copy(i - LAG_PLAIN):
+                stage(plain_products, i - LAG_PLAIN)
             stage(mx_products, n)
-            stage(gate_functions, n - LAG_GATES)
+            stage(sums, n - LAG_Z)
+            stage(gate_functions, n - LAG_Z)
             stage(two_products, n - LAG_GATES)
             stage(copy_x_t, i)
             stage(quantise, i - 1)
-            stage(copy_plain, i - 1)
-            stage(add_products, n)
+            stage(copy_mx, n)
             stage(new_c, n - LAG_C)
             stage(tanh_of_c, n - LAG_C)
             stage(new_h, n - LAG_H)

@@ -28,6 +28,7 @@ LAG_Z = 1
 LAG_GATES = 2
 LAG_C = 3
 LAG_H = 4
+V_UNITS = 3
 
 FLOPS = 2 * B * D * Z + 2 * B * U * Z
 
@@ -238,7 +239,7 @@ def tile_lstm_kernel(
                 nc.scalar.activation(out=z_sb[n][:, j, 3 * U : Z], in_=z_ps[n, j][:, 3 * U : Z], func=ACT.Tanh)
 
         def two_products(n):
-            engine = nc.gpsimd if n < UNITS - 1 else nc.vector
+            engine = nc.gpsimd if n < UNITS - V_UNITS else nc.vector
             z = z_sb[n]
             engine.tensor_tensor(out=kept[n][:], in0=z[:, :, U : 2 * U], in1=pre_c_sb[:, tiles_of(n), :], op=ALU.mult)
             engine.tensor_tensor(out=fresh[n][:], in0=z[:, :, 0:U], in1=z[:, :, 3 * U : Z], op=ALU.mult)

@@ -96,6 +96,7 @@ def tile_lstm_kernel(
         ident_f32 = keep.tile([P, P], F32)
         ident_bf16 = keep.tile([P, P], BF16)
         warm = keep.tile([P, 2], F32)
+        hold = keep.tile([P, 1], BF16)
 
         def tiles_of(n):
             return slice(n * UNIT, (n + 1) * UNIT)
@@ -106,7 +107,7 @@ def tile_lstm_kernel(
         nc.vector.memset(w_plane[:].bitcast(I32), 0)
         nc.vector.memset(warm[:, 0:1], 0.0)
         nc.vector.memset(ident_f32[:], 0.0)
-        load_x(nc.sync, 0)
+        load_x(nc.scalar, 0)
         for gate in range(GATES):
             nc.scalar.dma_start(out=u_sb[:, gate * U : (gate + 1) * U], in_=u_in[gate])
         nc.scalar.dma_start(out=pre_h_sb[:], in_=pre_h_view)
@@ -114,6 +115,7 @@ def tile_lstm_kernel(
         nc.scalar.activation(out=warm[:, 1:2], in_=warm[:, 0:1], func=ACT.Sigmoid)
         make_identity(nc, ident_f32[:], nomemset=True)
         nc.vector.tensor_copy(out=ident_bf16[:], in_=ident_f32[:])
+        nc.gpsimd.tensor_copy(out=hold[:], in_=x_sb[0][:, 0, 0:1])
         for n in range(2, TILES // CHUNK):
             load_x(nc.gpsimd, n)
         nc.gpsimd.dma_start(out=pre_c_sb[:], in_=pre_c_view)

@@ -19,7 +19,7 @@ Z = GATES * U
 TILES = B // P
 UNIT = 2
 UNITS = TILES // UNIT
-CHUNK = 4
+X_LOADS = (2, 2, 4, 4, 4)
 H_TILES = 8
 AHEAD = 6
 H_STEPS = (1, 3)
@@ -70,7 +70,12 @@ def tile_lstm_kernel(
         def per_unit(shape, dtype, name):
             return [keep.tile(shape, dtype, name="%s%d" % (name, n), align_bytes=64) for n in range(UNITS)]
 
-        x_sb = [keep.tile([P, CHUNK, D], BF16, name="x_sb%d" % n) for n in range(TILES // CHUNK)]
+        x_sb = [keep.tile([P, count, D], BF16, name="x_sb%d" % n) for n, count in enumerate(X_LOADS)]
+        x_first = [sum(X_LOADS[:n]) for n in range(len(X_LOADS))]
+        x_tile = {}
+        for n, count in enumerate(X_LOADS):
+            for j in range(count):
+                x_tile[x_first[n] + j] = x_sb[n][:, j, :]
         grouped = per_unit([P, UNIT, P, 4], BF16, "grouped")
         x_codes = per_unit([P, UNIT * P], U32, "x_codes")
         x_plane = per_unit([P, UNIT * P], U8, "x_plane")
@@ -102,21 +107,22 @@ def tile_lstm_kernel(
             return slice(n * UNIT, (n + 1) * UNIT)
 
         def load_x(queue, n):
-            queue.dma_start(out=x_sb[n][:], in_=x_view[:, n * CHUNK : (n + 1) * CHUNK, :])
+            queue.dma_start(out=x_sb[n][:], in_=x_view[:, x_first[n] : x_first[n] + X_LOADS[n], :])
 
         nc.vector.memset(w_plane[:].bitcast(I32), 0)
         nc.vector.memset(warm[:, 0:1], 0.0)
         nc.vector.memset(ident_f32[:], 0.0)
         load_x(nc.scalar, 0)
+        load_x(nc.scalar, 1)
         for gate in range(GATES):
             nc.scalar.dma_start(out=u_sb[:, gate * U : (gate + 1) * U], in_=u_in[gate])
         nc.scalar.dma_start(out=pre_h_sb[:], in_=pre_h_view)
-        load_x(nc.scalar, 1)
+        load_x(nc.scalar, 2)
         nc.scalar.activation(out=warm[:, 1:2], in_=warm[:, 0:1], func=ACT.Sigmoid)
         make_identity(nc, ident_f32[:], nomemset=True)
         nc.vector.tensor_copy(out=ident_bf16[:], in_=ident_f32[:])
         nc.gpsimd.tensor_copy(out=hold[:], in_=x_sb[0][:, 0, 0:1])
-        for n in range(2, TILES // CHUNK):
+        for n in range(3, len(X_LOADS)):
             load_x(nc.gpsimd, n)
         nc.gpsimd.dma_start(out=pre_c_sb[:], in_=pre_c_view)
         for gate in range(GATES):
@@ -135,7 +141,7 @@ def tile_lstm_kernel(
             xt_ps[n] = psum.tile([P, UNIT, 2, P], F32, name="xt%d" % n, tag="a", bufs=4)
             for j in range(UNIT):
                 t = n * UNIT + j
-                words = x_sb[t // CHUNK][:, t % CHUNK, :].bitcast(F32)
+                words = x_tile[t].bitcast(F32)
                 for u in range(2):
                     nc.tensor.transpose(xt_ps[n][:, j, u, :], words[:, u : D // 2 : 2], ident_f32[:])
 

@@ -21,14 +21,11 @@ UNIT = 2
 UNITS = TILES // UNIT
 X_LOADS = (2, 2, 4, 4, 4)
 H_TILES = 8
-AHEAD = 6
-H_STEPS = (1, 3)
-LAG_PLAIN = 2
 LAG_Z = 1
-LAG_GATES = 2
-LAG_C = 3
-LAG_H = 4
-V_UNITS = 3
+LAG_C = 2
+LAG_H = 3
+G_UNITS = ()
+S_X = (1, 3, 5, 7)
 
 FLOPS = 2 * B * D * Z + 2 * B * U * Z
 
@@ -91,7 +88,6 @@ def tile_lstm_kernel(
         ht_ps = {}
         y_ps = {}
         z_ps = {}
-        zp_ps = {}
 
         pre_h_sb = keep.tile([P, TILES, U], BF16)
         pre_c_sb = keep.tile([P, TILES, U], BF16)
@@ -101,7 +97,6 @@ def tile_lstm_kernel(
         ident_f32 = keep.tile([P, P], F32)
         ident_bf16 = keep.tile([P, P], BF16)
         warm = keep.tile([P, 2], F32)
-        hold = keep.tile([P, 1], BF16)
 
         def tiles_of(n):
             return slice(n * UNIT, (n + 1) * UNIT)
@@ -114,28 +109,26 @@ def tile_lstm_kernel(
         nc.vector.memset(ident_f32[:], 0.0)
         load_x(nc.scalar, 0)
         load_x(nc.scalar, 1)
-        for gate in range(GATES):
-            nc.scalar.dma_start(out=u_sb[:, gate * U : (gate + 1) * U], in_=u_in[gate])
-        nc.scalar.dma_start(out=pre_h_sb[:], in_=pre_h_view)
         load_x(nc.scalar, 2)
         nc.scalar.activation(out=warm[:, 1:2], in_=warm[:, 0:1], func=ACT.Sigmoid)
+        load_x(nc.gpsimd, 3)
         make_identity(nc, ident_f32[:], nomemset=True)
         nc.vector.tensor_copy(out=ident_bf16[:], in_=ident_f32[:])
-        nc.gpsimd.tensor_copy(out=hold[:], in_=x_sb[0][:, 0, 0:1])
-        for n in range(3, len(X_LOADS)):
-            load_x(nc.gpsimd, n)
+        nc.gpsimd.dma_start(out=pre_h_sb[:], in_=pre_h_view)
+        load_x(nc.gpsimd, 4)
         nc.gpsimd.dma_start(out=pre_c_sb[:], in_=pre_c_view)
+        for gate in range(GATES):
+            nc.sync.dma_start(
+                out=w_words[:, gate * U : (gate + 1) * U].bitcast(I32),
+                in_=w_words_in[gate].rearrange("o p n t -> (o p) (n t)").bitcast(I32),
+            )
         for gate in range(GATES):
             cols = slice(gate * U, (gate + 1) * U)
             rows = w_scales_in[gate].rearrange("o (q r) n -> r (o q) n", r=4).bitcast(I32)
             for r in range(4):
                 nc.sync.dma_start(out=w_plane[r:P:32, cols].bitcast(I32), in_=rows[r])
         for gate in range(GATES):
-            cols = slice(gate * U, (gate + 1) * U)
-            nc.sync.dma_start(
-                out=w_words[:, cols].bitcast(I32),
-                in_=w_words_in[gate].rearrange("o p n t -> (o p) (n t)").bitcast(I32),
-            )
+            nc.sync.dma_start(out=u_sb[:, gate * U : (gate + 1) * U], in_=u_in[gate])
 
         def transposes(n):
             xt_ps[n] = psum.tile([P, UNIT, 2, P], F32, name="xt%d" % n, tag="a", bufs=4)
@@ -152,7 +145,12 @@ def tile_lstm_kernel(
             nc.scalar.copy(out=pre_h_t[n][:], in_=ht_ps[n][:])
 
         def copy_x_t(n):
-            nc.vector.tensor_copy(out=grouped[n][:].bitcast(F32), in_=xt_ps[n][:].rearrange("p j u b -> p j b u"))
+            out = grouped[n][:].bitcast(F32)
+            in_ = xt_ps[n][:].rearrange("p j u b -> p j b u")
+            if n in S_X:
+                nc.scalar.copy(out=out, in_=in_)
+            else:
+                nc.vector.tensor_copy(out=out, in_=in_)
 
         def quantise(n):
             nc.vector.quantize_mx(
@@ -161,40 +159,7 @@ def tile_lstm_kernel(
                 in_=grouped[n][:].rearrange("p j b t -> p (j b t)"),
             )
 
-        def by_copy(n):
-            return n % 3 == 1
-
-        def plain_products(n):
-            for j in range(UNIT):
-                t = n * UNIT + j
-                zp_ps[n, j] = psum.tile([P, Z], F32, name="zp%d_%d" % (n, j), tag="z", bufs=4)
-                nc.tensor.matmul(
-                    out=zp_ps[n, j][:], lhsT=pre_h_t[t // H_TILES][:, t % H_TILES, :], rhs=u_sb[:], start=True, stop=True
-                )
-                nc.scalar.copy(out=z_sb[n][:, j, :], in_=zp_ps[n, j][:])
-
-        def mx_products_rows(n):
-            for j in range(UNIT):
-                cols = slice(j * P, (j + 1) * P)
-                z_ps[n, j] = psum.tile([P, Z], F32, name="zm%d_%d" % (n, j), tag="z", bufs=4)
-                nc.tensor.matmul_mx(
-                    out=z_ps[n, j][:],
-                    lhsT=x_codes[n][:, cols].bitcast(FP8X4),
-                    lhsT_scale=x_plane[n][:, cols],
-                    rhs=w_words[:].bitcast(FP8X4),
-                    rhs_scale=w_plane[:],
-                    start=True,
-                    stop=True,
-                )
-
-        def add_products(n):
-            for j in range(UNIT):
-                nc.vector.tensor_tensor(out=z_sb[n][:, j, :], in0=z_ps[n, j][:], in1=z_sb[n][:, j, :], op=ALU.add)
-
         def mx_products(n):
-            if by_copy(n):
-                mx_products_rows(n)
-                return
             for half in range(GATES // 2):
                 y_ps[n, half] = psum.tile([P, 2, UNIT * P], F32, name="y%d_%d" % (n, half), tag="a", bufs=4)
                 for e in range(2):
@@ -210,22 +175,21 @@ def tile_lstm_kernel(
                     )
 
         def copy_mx(n):
-            if by_copy(n):
-                add_products(n)
-                return
             for half in range(GATES // 2):
                 out = y_sb[n][:, 2 * half : 2 * half + 2, :, :].rearrange("p g j b -> p g (j b)")
-                nc.vector.tensor_copy(out=out, in_=y_ps[n, half][:])
+                if half == 0:
+                    nc.vector.tensor_copy(out=out, in_=y_ps[n, half][:])
+                else:
+                    nc.scalar.copy(out=out, in_=y_ps[n, half][:])
 
         def sums(n):
-            if by_copy(n):
-                return
             for j in range(UNIT):
                 t = n * UNIT + j
                 z_ps[n, j] = psum.tile([P, Z], F32, name="z%d_%d" % (n, j), tag="z", bufs=4)
                 nc.tensor.matmul(
                     out=z_ps[n, j][:], lhsT=pre_h_t[t // H_TILES][:, t % H_TILES, :], rhs=u_sb[:], start=True, stop=False
                 )
+            for j in range(UNIT):
                 for gate in range(GATES):
                     nc.tensor.matmul(
                         out=z_ps[n, j][:, gate * U : (gate + 1) * U],
@@ -237,17 +201,12 @@ def tile_lstm_kernel(
                     )
 
         def gate_functions(n):
-            if by_copy(n):
-                z = z_sb[n]
-                nc.scalar.activation(out=z[:, :, 0 : 3 * U], in_=z[:, :, 0 : 3 * U], func=ACT.Sigmoid)
-                nc.scalar.activation(out=z[:, :, 3 * U : Z], in_=z[:, :, 3 * U : Z], func=ACT.Tanh)
-                return
             for j in range(UNIT):
                 nc.scalar.activation(out=z_sb[n][:, j, 0 : 3 * U], in_=z_ps[n, j][:, 0 : 3 * U], func=ACT.Sigmoid)
                 nc.scalar.activation(out=z_sb[n][:, j, 3 * U : Z], in_=z_ps[n, j][:, 3 * U : Z], func=ACT.Tanh)
 
         def two_products(n):
-            engine = nc.gpsimd if n < UNITS - V_UNITS else nc.vector
+            engine = nc.gpsimd if n in G_UNITS else nc.vector
             z = z_sb[n]
             engine.tensor_tensor(out=kept[n][:], in0=z[:, :, U : 2 * U], in1=pre_c_sb[:, tiles_of(n), :], op=ALU.mult)
             engine.tensor_tensor(out=fresh[n][:], in0=z[:, :, 0:U], in1=z[:, :, 3 * U : Z], op=ALU.mult)
@@ -267,20 +226,20 @@ def tile_lstm_kernel(
             if 0 <= n < UNITS:
                 work(n)
 
-        for i in range(UNITS + AHEAD + LAG_H + 1):
-            n = i - AHEAD
-            stage(transposes, i)
-            if i in H_STEPS:
-                transposes_h(H_STEPS.index(i))
-            if by_copy(i - LAG_PLAIN):
-                stage(plain_products, i - LAG_PLAIN)
+        for n in range(UNITS + 1):
+            if n == 6:
+                for half in range(TILES // H_TILES):
+                    transposes_h(half)
+            stage(transposes, n)
+            stage(copy_x_t, n)
+            stage(quantise, n - 1)
+
+        for n in range(UNITS + LAG_H + 1):
             stage(mx_products, n)
             stage(sums, n - LAG_Z)
-            stage(gate_functions, n - LAG_Z)
-            stage(two_products, n - LAG_GATES)
-            stage(copy_x_t, i)
-            stage(quantise, i - 1)
             stage(copy_mx, n)
-            stage(new_c, n - LAG_C)
-            stage(tanh_of_c, n - LAG_C)
+            stage(tanh_of_c, n - LAG_H)
+            stage(gate_functions, n - LAG_Z)
+            stage(two_products, n - LAG_C)
             stage(new_h, n - LAG_H)
+            stage(new_c, n - LAG_C)

@@ -21,11 +21,12 @@ UNIT = 2
 UNITS = TILES // UNIT
 X_LOADS = (2, 2, 4, 4, 4)
 H_TILES = 8
+V_Y = (2, 5)
 LAG_Z = 1
 LAG_C = 2
 LAG_H = 3
 G_UNITS = ()
-S_X = (1, 3, 5, 7)
+S_X = (1, 3, 4, 6, 7)
 
 FLOPS = 2 * B * D * Z + 2 * B * U * Z
 
@@ -114,8 +115,8 @@ def tile_lstm_kernel(
         load_x(nc.gpsimd, 3)
         make_identity(nc, ident_f32[:], nomemset=True)
         nc.vector.tensor_copy(out=ident_bf16[:], in_=ident_f32[:])
-        nc.gpsimd.dma_start(out=pre_h_sb[:], in_=pre_h_view)
         load_x(nc.gpsimd, 4)
+        nc.gpsimd.dma_start(out=pre_h_sb[:], in_=pre_h_view)
         nc.gpsimd.dma_start(out=pre_c_sb[:], in_=pre_c_view)
         for gate in range(GATES):
             nc.sync.dma_start(
@@ -142,7 +143,7 @@ def tile_lstm_kernel(
             ht_ps[n] = psum.tile([P, H_TILES, P], BF16, name="ht%d" % n, tag="a", bufs=4)
             for j in range(H_TILES):
                 nc.tensor.transpose(ht_ps[n][:, j, :], pre_h_sb[:, n * H_TILES + j, :], ident_bf16[:])
-            nc.scalar.copy(out=pre_h_t[n][:], in_=ht_ps[n][:])
+            nc.vector.tensor_copy(out=pre_h_t[n][:], in_=ht_ps[n][:])
 
         def copy_x_t(n):
             out = grouped[n][:].bitcast(F32)
@@ -177,7 +178,7 @@ def tile_lstm_kernel(
         def copy_mx(n):
             for half in range(GATES // 2):
                 out = y_sb[n][:, 2 * half : 2 * half + 2, :, :].rearrange("p g j b -> p g (j b)")
-                if half == 0:
+                if half == 0 or n in V_Y:
                     nc.vector.tensor_copy(out=out, in_=y_ps[n, half][:])
                 else:
                     nc.scalar.copy(out=out, in_=y_ps[n, half][:])
@@ -227,7 +228,7 @@ def tile_lstm_kernel(
                 work(n)
 
         for n in range(UNITS + 1):
-            if n == 6:
+            if n == UNITS:
                 for half in range(TILES // H_TILES):
                     transposes_h(half)
             stage(transposes, n)

@@ -98,6 +98,7 @@ def tile_lstm_kernel(
         ident_f32 = keep.tile([P, P], F32)
         ident_bf16 = keep.tile([P, P], BF16)
         warm = keep.tile([P, 2], F32)
+        hold = keep.tile([P, 1], BF16)
 
         def tiles_of(n):
             return slice(n * UNIT, (n + 1) * UNIT)
@@ -111,23 +112,24 @@ def tile_lstm_kernel(
         load_x(nc.scalar, 0)
         load_x(nc.scalar, 1)
         load_x(nc.scalar, 2)
+        load_x(nc.scalar, 3)
         nc.scalar.activation(out=warm[:, 1:2], in_=warm[:, 0:1], func=ACT.Sigmoid)
-        load_x(nc.gpsimd, 3)
         make_identity(nc, ident_f32[:], nomemset=True)
         nc.vector.tensor_copy(out=ident_bf16[:], in_=ident_f32[:])
-        load_x(nc.gpsimd, 4)
+        nc.gpsimd.tensor_copy(out=hold[:], in_=x_sb[0][:, 0, 0:1])
         nc.gpsimd.dma_start(out=pre_h_sb[:], in_=pre_h_view)
+        load_x(nc.gpsimd, 4)
         nc.gpsimd.dma_start(out=pre_c_sb[:], in_=pre_c_view)
-        for gate in range(GATES):
-            nc.sync.dma_start(
-                out=w_words[:, gate * U : (gate + 1) * U].bitcast(I32),
-                in_=w_words_in[gate].rearrange("o p n t -> (o p) (n t)").bitcast(I32),
-            )
         for gate in range(GATES):
             cols = slice(gate * U, (gate + 1) * U)
             rows = w_scales_in[gate].rearrange("o (q r) n -> r (o q) n", r=4).bitcast(I32)
             for r in range(4):
                 nc.sync.dma_start(out=w_plane[r:P:32, cols].bitcast(I32), in_=rows[r])
+        for gate in range(GATES):
+            nc.sync.dma_start(
+                out=w_words[:, gate * U : (gate + 1) * U].bitcast(I32),
+                in_=w_words_in[gate].rearrange("o p n t -> (o p) (n t)").bitcast(I32),
+            )
         for gate in range(GATES):
             nc.sync.dma_start(out=u_sb[:, gate * U : (gate + 1) * U], in_=u_in[gate])
 
@@ -228,7 +230,7 @@ def tile_lstm_kernel(
                 work(n)
 
         for n in range(UNITS + 1):
-            if n == UNITS:
+            if n == 6:
                 for half in range(TILES // H_TILES):
                     transposes_h(half)
             stage(transposes, n)

@@ -119,6 +119,8 @@ def tile_lstm_kernel(
         nc.gpsimd.tensor_copy(out=hold[:], in_=x_sb[0][:, 0, 0:1])
         nc.gpsimd.dma_start(out=pre_h_sb[:], in_=pre_h_view)
         load_x(nc.gpsimd, 4)
+        for gate in range(GATES):
+            nc.gpsimd.dma_start(out=u_sb[:, gate * U : (gate + 1) * U], in_=u_in[gate])
         nc.gpsimd.dma_start(out=pre_c_sb[:], in_=pre_c_view)
         for gate in range(GATES):
             cols = slice(gate * U, (gate + 1) * U)
@@ -130,8 +132,6 @@ def tile_lstm_kernel(
                 out=w_words[:, gate * U : (gate + 1) * U].bitcast(I32),
                 in_=w_words_in[gate].rearrange("o p n t -> (o p) (n t)").bitcast(I32),
             )
-        for gate in range(GATES):
-            nc.sync.dma_start(out=u_sb[:, gate * U : (gate + 1) * U], in_=u_in[gate])
 
         def transposes(n):
             xt_ps[n] = psum.tile([P, UNIT, 2, P], F32, name="xt%d" % n, tag="a", bufs=4)

from contextlib import ExitStack

import concourse.mybir as mybir
from concourse.masks import make_identity

F32 = mybir.dt.float32
BF16 = mybir.dt.bfloat16
I32 = mybir.dt.int32
U32 = mybir.dt.uint32
U8 = mybir.dt.uint8
FP8X4 = mybir.dt.float8_e4m3fn_x4
ACT = mybir.ActivationFunctionType
ALU = mybir.AluOpType

P = 128
B, D, U = 2048, 512, 128
GATES = 4
Z = GATES * U
TILES = B // P
UNIT = 2
UNITS = TILES // UNIT
X_LOADS = (2, 2, 4, 4, 4)
H_TILES = 8
V_Y = (2, 5)
LAG_Z = 1
LAG_C = 2
LAG_H = 3
G_UNITS = ()
S_X = (1, 3, 4, 6, 7)

FLOPS = 2 * B * D * Z + 2 * B * U * Z


def tile_lstm_kernel(
    tc,
    pre_layer,
    x,
    W_i_words,
    W_i_scales,
    W_f_words,
    W_f_scales,
    W_o_words,
    W_o_scales,
    W_c_words,
    W_c_scales,
    U_i,
    U_f,
    U_o,
    U_c,
    out,
):
    nc = tc.nc
    w_words_in = [W_i_words, W_f_words, W_o_words, W_c_words]
    w_scales_in = [W_i_scales, W_f_scales, W_o_scales, W_c_scales]
    u_in = [U_i, U_f, U_o, U_c]

    x_view = x.rearrange("(p t) k -> p t k", t=TILES)
    pre_h_view = pre_layer[0].rearrange("(p t) u -> p t u", t=TILES)
    pre_c_view = pre_layer[1].rearrange("(p t) u -> p t u", t=TILES)
    h_view = out[0].rearrange("(p t) u -> p t u", t=TILES)
    c_view = out[1].rearrange("(p t) u -> p t u", t=TILES)

    with ExitStack() as ctx:
        ctx.enter_context(tc.manual_schedule())
        keep = ctx.enter_context(tc.tile_pool(name="keep", bufs=1))
        psum = ctx.enter_context(tc.psum_pool(name="psum", bufs=1))

        def per_unit(shape, dtype, name):
            return [keep.tile(shape, dtype, name="%s%d" % (name, n), align_bytes=64) for n in range(UNITS)]

        x_sb = [keep.tile([P, count, D], BF16, name="x_sb%d" % n) for n, count in enumerate(X_LOADS)]
        x_first = [sum(X_LOADS[:n]) for n in range(len(X_LOADS))]
        x_tile = {}
        for n, count in enumerate(X_LOADS):
            for j in range(count):
                x_tile[x_first[n] + j] = x_sb[n][:, j, :]
        grouped = per_unit([P, UNIT, P, 4], BF16, "grouped")
        x_codes = per_unit([P, UNIT * P], U32, "x_codes")
        x_plane = per_unit([P, UNIT * P], U8, "x_plane")
        pre_h_t = [keep.tile([P, H_TILES, P], BF16, name="pre_h_t%d" % n) for n in range(TILES // H_TILES)]
        y_sb = per_unit([P, GATES, UNIT, P], F32, "y_sb")
        z_sb = per_unit([P, UNIT, Z], F32, "z_sb")
        kept = per_unit([P, UNIT, U], F32, "kept")
        fresh = per_unit([P, UNIT, U], F32, "fresh")
        c_sb = per_unit([P, UNIT, U], F32, "c_sb")
        tanh_c = per_unit([P, UNIT, U], F32, "tanh_c")
        h_sb = per_unit([P, UNIT, U], F32, "h_sb")
        xt_ps = {}
        ht_ps = {}
        y_ps = {}
        z_ps = {}

        pre_h_sb = keep.tile([P, TILES, U], BF16)
        pre_c_sb = keep.tile([P, TILES, U], BF16)
        u_sb = keep.tile([P, Z], BF16)
        w_words = keep.tile([P, Z], U32, align_bytes=64)
        w_plane = keep.tile([P, Z], U8, align_bytes=64)
        ident_f32 = keep.tile([P, P], F32)
        ident_bf16 = keep.tile([P, P], BF16)
        warm = keep.tile([P, 2], F32)
        hold = keep.tile([P, 1], BF16)

        def tiles_of(n):
            return slice(n * UNIT, (n + 1) * UNIT)

        def load_x(queue, n):
            queue.dma_start(out=x_sb[n][:], in_=x_view[:, x_first[n] : x_first[n] + X_LOADS[n], :])

        nc.vector.memset(w_plane[:].bitcast(I32), 0)
        nc.vector.memset(warm[:, 0:1], 0.0)
        nc.vector.memset(ident_f32[:], 0.0)
        load_x(nc.scalar, 0)
        load_x(nc.scalar, 1)
        load_x(nc.scalar, 2)
        load_x(nc.scalar, 3)
        nc.scalar.activation(out=warm[:, 1:2], in_=warm[:, 0:1], func=ACT.Sigmoid)
        make_identity(nc, ident_f32[:], nomemset=True)
        nc.vector.tensor_copy(out=ident_bf16[:], in_=ident_f32[:])
        nc.gpsimd.tensor_copy(out=hold[:], in_=x_sb[0][:, 0, 0:1])
        nc.gpsimd.dma_start(out=pre_h_sb[:], in_=pre_h_view)
        load_x(nc.gpsimd, 4)
        for gate in range(GATES):
            nc.gpsimd.dma_start(out=u_sb[:, gate * U : (gate + 1) * U], in_=u_in[gate])
        nc.gpsimd.dma_start(out=pre_c_sb[:], in_=pre_c_view)
        for gate in range(GATES):
            cols = slice(gate * U, (gate + 1) * U)
            rows = w_scales_in[gate].rearrange("o (q r) n -> r (o q) n", r=4).bitcast(I32)
            for r in range(4):
                nc.sync.dma_start(out=w_plane[r:P:32, cols].bitcast(I32), in_=rows[r])
        for gate in range(GATES):
            nc.sync.dma_start(
                out=w_words[:, gate * U : (gate + 1) * U].bitcast(I32),
                in_=w_words_in[gate].rearrange("o p n t -> (o p) (n t)").bitcast(I32),
            )

        def transposes(n):
            xt_ps[n] = psum.tile([P, UNIT, 2, P], F32, name="xt%d" % n, tag="a", bufs=4)
            for j in range(UNIT):
                t = n * UNIT + j
                words = x_tile[t].bitcast(F32)
                for u in range(2):
                    nc.tensor.transpose(xt_ps[n][:, j, u, :], words[:, u : D // 2 : 2], ident_f32[:])

        def transposes_h(n):
            ht_ps[n] = psum.tile([P, H_TILES, P], BF16, name="ht%d" % n, tag="a", bufs=4)
            for j in range(H_TILES):
                nc.tensor.transpose(ht_ps[n][:, j, :], pre_h_sb[:, n * H_TILES + j, :], ident_bf16[:])
            nc.vector.tensor_copy(out=pre_h_t[n][:], in_=ht_ps[n][:])

        def copy_x_t(n):
            out = grouped[n][:].bitcast(F32)
            in_ = xt_ps[n][:].rearrange("p j u b -> p j b u")
            if n in S_X:
                nc.scalar.copy(out=out, in_=in_)
            else:
                nc.vector.tensor_copy(out=out, in_=in_)

        def quantise(n):
            nc.vector.quantize_mx(
                out=x_codes[n][:].bitcast(FP8X4),
                scales=x_plane[n][:],
                in_=grouped[n][:].rearrange("p j b t -> p (j b t)"),
            )

        def mx_products(n):
            for half in range(GATES // 2):
                y_ps[n, half] = psum.tile([P, 2, UNIT * P], F32, name="y%d_%d" % (n, half), tag="a", bufs=4)
                for e in range(2):
                    cols = slice((2 * half + e) * U, (2 * half + e + 1) * U)
                    nc.tensor.matmul_mx(
                        out=y_ps[n, half][:, e, :],
                        lhsT=w_words[:, cols].bitcast(FP8X4),
                        lhsT_scale=w_plane[:, cols],
                        rhs=x_codes[n][:].bitcast(FP8X4),
                        rhs_scale=x_plane[n][:],
                        start=True,
                        stop=True,
                    )

        def copy_mx(n):
            for half in range(GATES // 2):
                out = y_sb[n][:, 2 * half : 2 * half + 2, :, :].rearrange("p g j b -> p g (j b)")
                if half == 0 or n in V_Y:
                    nc.vector.tensor_copy(out=out, in_=y_ps[n, half][:])
                else:
                    nc.scalar.copy(out=out, in_=y_ps[n, half][:])

        def sums(n):
            for j in range(UNIT):
                t = n * UNIT + j
                z_ps[n, j] = psum.tile([P, Z], F32, name="z%d_%d" % (n, j), tag="z", bufs=4)
                nc.tensor.matmul(
                    out=z_ps[n, j][:], lhsT=pre_h_t[t // H_TILES][:, t % H_TILES, :], rhs=u_sb[:], start=True, stop=False
                )
            for j in range(UNIT):
                for gate in range(GATES):
                    nc.tensor.matmul(
                        out=z_ps[n, j][:, gate * U : (gate + 1) * U],
                        lhsT=y_sb[n][:, gate, j, :],
                        rhs=ident_f32[:],
                        is_transpose=True,
                        start=False,
                        stop=(gate == GATES - 1),
                    )

        def gate_functions(n):
            for j in range(UNIT):
                nc.scalar.activation(out=z_sb[n][:, j, 0 : 3 * U], in_=z_ps[n, j][:, 0 : 3 * U], func=ACT.Sigmoid)
                nc.scalar.activation(out=z_sb[n][:, j, 3 * U : Z], in_=z_ps[n, j][:, 3 * U : Z], func=ACT.Tanh)

        def two_products(n):
            engine = nc.gpsimd if n in G_UNITS else nc.vector
            z = z_sb[n]
            engine.tensor_tensor(out=kept[n][:], in0=z[:, :, U : 2 * U], in1=pre_c_sb[:, tiles_of(n), :], op=ALU.mult)
            engine.tensor_tensor(out=fresh[n][:], in0=z[:, :, 0:U], in1=z[:, :, 3 * U : Z], op=ALU.mult)

        def new_c(n):
            nc.vector.tensor_tensor(out=c_sb[n][:], in0=kept[n][:], in1=fresh[n][:], op=ALU.add)
            nc.sync.dma_start(out=c_view[:, tiles_of(n), :], in_=c_sb[n][:])

        def tanh_of_c(n):
            nc.scalar.activation(out=tanh_c[n][:], in_=c_sb[n][:], func=ACT.Tanh)

        def new_h(n):
            nc.vector.tensor_tensor(out=h_sb[n][:], in0=z_sb[n][:, :, 2 * U : 3 * U], in1=tanh_c[n][:], op=ALU.mult)
            nc.sync.dma_start(out=h_view[:, tiles_of(n), :], in_=h_sb[n][:])

        def stage(work, n):
            if 0 <= n < UNITS:
                work(n)

        for n in range(UNITS + 1):
            if n == 6:
                for half in range(TILES // H_TILES):
                    transposes_h(half)
            stage(transposes, n)
            stage(copy_x_t, n)
            stage(quantise, n - 1)

        for n in range(UNITS + LAG_H + 1):
            stage(mx_products, n)
            stage(sums, n - LAG_Z)
            stage(copy_mx, n)
            stage(tanh_of_c, n - LAG_H)
            stage(gate_functions, n - LAG_Z)
            stage(two_products, n - LAG_C)
            stage(new_h, n - LAG_H)
            stage(new_c, n - LAG_C)
